import numpy as np
import ml_dtypes


def mxq(x, axis, fmt="e4m3"):
    dtype, down = {"e4m3": (ml_dtypes.float8_e4m3fn, 7), "e5m2": (ml_dtypes.float8_e5m2, 14)}[fmt]
    v = np.moveaxis(np.asarray(x, np.float32).astype(ml_dtypes.bfloat16).astype(np.float64), axis, -1)
    blocks = v.reshape(v.shape[:-1] + (-1, 32))
    amax = np.abs(blocks).max(-1, keepdims=True)
    byte = np.maximum(np.where(amax > 0, np.frexp(amax)[1] - 1 + 127, 0) - down, 1)
    scale = np.exp2(byte - 127.0)
    codes = (blocks / scale).astype(np.float32).astype(dtype).astype(np.float64)
    return np.moveaxis((codes * scale).reshape(v.shape), -1, axis)


WIDE = False


def mx_kscale(k):
    if not WIDE:
        return np.ones(k)
    levels = np.array([10, -10, 5, -5, 0])
    a = np.random.permutation(np.resize(levels, k // 512 * 4)).reshape(k // 512, 4)
    idx = np.arange(k)
    return np.exp2(a[idx // 512, idx % 128 // 32])


BF16 = ml_dtypes.bfloat16


def bf(x):
    return np.asarray(x, np.float32).astype(BF16)


def f64(x):
    return np.asarray(x).astype(np.float64)


B, N, D, H, E, O = 1, 512, 512, 4, 2048, 2048


def setup_inputs():
    s = mx_kscale(E)
    g = np.sqrt(2.0 / np.sqrt(D)) / np.sqrt(E)
    return {"x": bf(np.random.standard_normal((B, N, E)) * s),
            "w_q": bf(np.random.standard_normal((H * D, E)) * g / s),
            "w_k": bf(np.random.standard_normal((H * D, E)) * g / s)}


def reference(x, w_q, w_k):
    xq = mxq(f64(x), 2, "e4m3")
    q = (xq @ mxq(f64(w_q), 1, "e4m3").T).reshape(B, N, H, D).transpose(0, 2, 1, 3)
    k = (xq @ mxq(f64(w_k), 1, "e4m3").T).reshape(B, N, H, D).transpose(0, 2, 1, 3)
    return mxq(q, 3, "e4m3") @ mxq(k, 2, "e4m3")

@@ -1,0 +1,182 @@
+from contextlib import ExitStack
+
+import concourse.mybir as mybir
+from concourse.masks import make_identity
+
+BF16 = mybir.dt.bfloat16
+F32 = mybir.dt.float32
+U32 = mybir.dt.uint32
+U8 = mybir.dt.uint8
+FP8X4 = mybir.dt.float8_e4m3fn_x4
+
+P = 128
+PACK = 4
+K_PASS = P * PACK
+TOKENS = 512
+MODEL = 2048
+HEADS = 4
+HEAD = 512
+PASSES = MODEL // K_PASS
+SLOTS = 2
+UNIT = SLOTS * P
+HALVES = HEAD // UNIT
+WORD_PLANES = 2
+
+FLOPS = 2 * 2 * TOKENS * MODEL * HEADS * HEAD + 2 * HEADS * TOKENS * HEAD * TOKENS
+
+
+def tile_attention_pa_kernel(tc, x, w_q, w_k, out):
+    nc = tc.nc
+
+    x_units = x[0].rearrange("(p half s) e -> half p s e", half=HALVES, s=SLOTS)
+    q_units = w_q.rearrange("(h p half s) e -> h half p s e", h=HEADS, half=HALVES, s=SLOTS)
+    k_units = w_k.rearrange("(h half s p) e -> h half p s e", h=HEADS, half=HALVES, s=SLOTS)
+    out_rows = out[0].rearrange("h (c t) m -> h c t m", t=PACK)
+
+    with ExitStack() as ctx:
+        consts = ctx.enter_context(tc.tile_pool(name="consts", bufs=1))
+        raw_pool = ctx.enter_context(tc.tile_pool(name="raw", bufs=HALVES * (1 + 2 * HEADS)))
+        stage = ctx.enter_context(tc.tile_pool(name="stage", bufs=6))
+        w_pool = ctx.enter_context(tc.tile_pool(name="w", bufs=3))
+        qk_pool = ctx.enter_context(tc.tile_pool(name="qk", bufs=2))
+        out_pool = ctx.enter_context(tc.tile_pool(name="outs", bufs=3))
+        turn_psum = ctx.enter_context(tc.psum_pool(name="turn", bufs=4))
+        acc_psum = ctx.enter_context(tc.psum_pool(name="acc", bufs=4))
+        ctx.enter_context(tc.manual_schedule())
+
+        ident = consts.tile([P, P], F32)
+        make_identity(nc, ident[:])
+        x_codes = consts.tile([P, PASSES, TOKENS], U32, align_bytes=64)
+        x_scales = consts.tile([P, PASSES, TOKENS], U8, align_bytes=64)
+
+        def load(rows):
+            raw = raw_pool.tile([P, SLOTS, MODEL], BF16)
+            nc.sync.dma_start(out=raw[:], in_=rows)
+            return raw
+
+        def transpose_and_quantise(raw, codes, scales):
+            for g in range(PASSES):
+                turned = turn_psum.tile([P, SLOTS, WORD_PLANES, P], F32)
+                for s in range(SLOTS):
+                    words = raw[:, s, :].bitcast(F32)
+                    for u in range(WORD_PLANES):
+                        first = (WORD_PLANES * g + u) * P
+                        nc.tensor.transpose(turned[:, s, u, :], words[:, first : first + P], ident[:])
+                grouped = stage.tile([P, UNIT * PACK], BF16, align_bytes=64)
+                nc.scalar.copy(
+                    out=grouped[:].bitcast(F32).rearrange("p (s r u) -> p s r u", s=SLOTS, u=WORD_PLANES),
+                    in_=turned[:].rearrange("p s u r -> p s r u"),
+                )
+                nc.vector.quantize_mx(out=codes[:, g, :].bitcast(FP8X4), scales=scales[:, g, :], in_=grouped[:])
+
+        def project(acc, lhs, lhs_cols, rhs, rhs_cols):
+            lhs_codes, lhs_scales = lhs
+            rhs_codes, rhs_scales = rhs
+            for g in range(PASSES):
+                nc.tensor.matmul_mx(
+                    out=acc,
+                    lhsT=lhs_codes[:, g, lhs_cols].bitcast(FP8X4),
+                    lhsT_scale=lhs_scales[:, g, lhs_cols],
+                    rhs=rhs_codes[:, g, rhs_cols].bitcast(FP8X4),
+                    rhs_scale=rhs_scales[:, g, rhs_cols],
+                    start=(g == 0),
+                    stop=(g == PASSES - 1),
+                )
+
+        def slot_cols(t):
+            return slice(t * P, (t + 1) * P)
+
+        def unit_cols(half):
+            return slice(half * UNIT, (half + 1) * UNIT)
+
+        x_mx = (x_codes, x_scales)
+
+        def project_q(w_mx, q_grouped, half):
+            for token_half in range(HALVES):
+                acc = acc_psum.tile([P, SLOTS, UNIT], F32)
+                for s in range(SLOTS):
+                    project(acc[:, s, :], w_mx, slot_cols(s), x_mx, unit_cols(token_half))
+                nc.vector.tensor_copy(
+                    out=q_grouped[:, unit_cols(token_half), SLOTS * half : SLOTS * (half + 1)],
+                    in_=acc[:].rearrange("p s n -> p n s"),
+                )
+
+        def project_k(w_mx, k_grouped):
+            for pair in range(PACK // SLOTS):
+                acc = acc_psum.tile([P, SLOTS, UNIT], F32)
+                for s in range(SLOTS):
+                    project(acc[:, s, :], x_mx, slot_cols(SLOTS * pair + s), w_mx, unit_cols(0))
+                nc.vector.tensor_copy(
+                    out=k_grouped[:, :, SLOTS * pair : SLOTS * (pair + 1)],
+                    in_=acc[:].rearrange("p s m -> p m s"),
+                )
+
+        def quantise_grouped(grouped, width):
+            codes = qk_pool.tile([P, width], U32, align_bytes=64, name="codes%d" % width)
+            scales = qk_pool.tile([P, width], U8, align_bytes=64, name="scales%d" % width)
+            nc.vector.quantize_mx(
+                out=codes[:].bitcast(FP8X4), scales=scales[:], in_=grouped[:].rearrange("p n t -> p (n t)")
+            )
+            return codes, scales
+
+        def logits(q_mx, k_mx, h, half):
+            q_codes, q_scales = q_mx
+            k_codes, k_scales = k_mx
+            result = out_pool.tile([P, PACK, UNIT], F32)
+            for pair in range(PACK // SLOTS):
+                acc = acc_psum.tile([P, SLOTS, UNIT], F32)
+                for s in range(SLOTS):
+                    cols = slot_cols(SLOTS * pair + s)
+                    nc.tensor.matmul_mx(
+                        out=acc[:, s, :],
+                        lhsT=q_codes[:, cols].bitcast(FP8X4),
+                        lhsT_scale=q_scales[:, cols],
+                        rhs=k_codes[:].bitcast(FP8X4),
+                        rhs_scale=k_scales[:],
+                        start=True,
+                        stop=True,
+                    )
+                nc.scalar.copy(out=result[:, SLOTS * pair : SLOTS * (pair + 1), :], in_=acc[:])
+            nc.sync.dma_start(out=out_rows[h][:, :, unit_cols(half)], in_=result[:])
+
+        x_raw = [load(x_units[half]) for half in range(HALVES)]
+        units = []
+        for h in range(HEADS):
+            for half in range(HALVES):
+                units.append((True, h, half, load(q_units[h, half])))
+            for half in range(HALVES):
+                units.append((False, h, half, load(k_units[h, half])))
+
+        def prepare(unit):
+            w_codes = w_pool.tile([P, PASSES, UNIT], U32, align_bytes=64)
+            w_scales = w_pool.tile([P, PASSES, UNIT], U8, align_bytes=64)
+            transpose_and_quantise(unit[3], w_codes, w_scales)
+            return w_codes, w_scales
+
+        for half in range(HALVES):
+            transpose_and_quantise(x_raw[half], x_codes[:, :, unit_cols(half)], x_scales[:, :, unit_cols(half)])
+
+        ready = prepare(units[0])
+        waiting = None
+        q_grouped = None
+        q_mx = None
+        for i, (is_q, h, half, raw) in enumerate(units):
+            w_mx = ready
+            if i + 1 < len(units):
+                ready = prepare(units[i + 1])
+            if is_q:
+                if half == 0:
+                    q_grouped = qk_pool.tile([P, TOKENS, PACK], BF16, align_bytes=64)
+                project_q(w_mx, q_grouped, half)
+                if half == HALVES - 1:
+                    q_mx = quantise_grouped(q_grouped, TOKENS)
+            else:
+                k_grouped = qk_pool.tile([P, UNIT, PACK], BF16, align_bytes=64)
+                project_k(w_mx, k_grouped)
+                k_mx = quantise_grouped(k_grouped, UNIT)
+            if waiting is not None:
+                logits(*waiting)
+                waiting = None
+            if not is_q:
+                waiting = (q_mx, k_mx, h, half)
+        logits(*waiting)

@@ -20,6 +20,8 @@ PASSES = MODEL // K_PASS
 SLOTS = 2
 UNIT = SLOTS * P
 HALVES = HEAD // UNIT
+WARM_START = 8
+WARM_UNIT = 2
 WORD_PLANES = 2
 
 FLOPS = 2 * 2 * TOKENS * MODEL * HEADS * HEAD + 2 * HEADS * TOKENS * HEAD * TOKENS
@@ -48,6 +50,14 @@ def tile_attention_pa_kernel(tc, x, w_q, w_k, out):
         make_identity(nc, ident[:])
         x_codes = consts.tile([P, PASSES, TOKENS], U32, align_bytes=64)
         x_scales = consts.tile([P, PASSES, TOKENS], U8, align_bytes=64)
+
+        zeros = consts.tile([P, HEAD], BF16)
+        nc.vector.memset(zeros[:], 0.0)
+
+        def keep_warm(count):
+            for c in range(count):
+                spare = acc_psum.tile([P, HEAD], F32, name="acc")
+                nc.tensor.matmul(spare[:], zeros[:, :P], zeros[:], start=True, stop=True)
 
         def load(rows):
             raw = raw_pool.tile([P, SLOTS, MODEL], BF16)
@@ -93,7 +103,7 @@ def tile_attention_pa_kernel(tc, x, w_q, w_k, out):
 
         def project_q(w_mx, q_grouped, half):
             for token_half in range(HALVES):
-                acc = acc_psum.tile([P, SLOTS, UNIT], F32)
+                acc = acc_psum.tile([P, SLOTS, UNIT], F32, name="acc")
                 for s in range(SLOTS):
                     project(acc[:, s, :], w_mx, slot_cols(s), x_mx, unit_cols(token_half))
                 nc.vector.tensor_copy(
@@ -103,7 +113,7 @@ def tile_attention_pa_kernel(tc, x, w_q, w_k, out):
 
         def project_k(w_mx, k_grouped):
             for pair in range(PACK // SLOTS):
-                acc = acc_psum.tile([P, SLOTS, UNIT], F32)
+                acc = acc_psum.tile([P, SLOTS, UNIT], F32, name="acc")
                 for s in range(SLOTS):
                     project(acc[:, s, :], x_mx, slot_cols(SLOTS * pair + s), w_mx, unit_cols(0))
                 nc.vector.tensor_copy(
@@ -124,7 +134,7 @@ def tile_attention_pa_kernel(tc, x, w_q, w_k, out):
             k_codes, k_scales = k_mx
             result = out_pool.tile([P, PACK, UNIT], F32)
             for pair in range(PACK // SLOTS):
-                acc = acc_psum.tile([P, SLOTS, UNIT], F32)
+                acc = acc_psum.tile([P, SLOTS, UNIT], F32, name="acc")
                 for s in range(SLOTS):
                     cols = slot_cols(SLOTS * pair + s)
                     nc.tensor.matmul_mx(
@@ -153,10 +163,13 @@ def tile_attention_pa_kernel(tc, x, w_q, w_k, out):
             transpose_and_quantise(unit[3], w_codes, w_scales)
             return w_codes, w_scales
 
+        keep_warm(WARM_START)
         for half in range(HALVES):
             transpose_and_quantise(x_raw[half], x_codes[:, :, unit_cols(half)], x_scales[:, :, unit_cols(half)])
+            keep_warm(WARM_UNIT)
 
         ready = prepare(units[0])
+        keep_warm(WARM_UNIT)
         waiting = None
         q_grouped = None
         q_mx = None

@@ -19,9 +19,13 @@ HEAD = 512
 PASSES = MODEL // K_PASS
 SLOTS = 2
 UNIT = SLOTS * P
+X_ROW = TOKENS + TOKENS // 4
 HALVES = HEAD // UNIT
-WARM_START = 8
-WARM_UNIT = 2
+RAW_BUFS = 18
+SHARE = (1,)
+S_COPY_K = ()
+S_COPY_Q = ()
+WARM = (6, 0)
 WORD_PLANES = 2
 
 FLOPS = 2 * 2 * TOKENS * MODEL * HEADS * HEAD + 2 * HEADS * TOKENS * HEAD * TOKENS
@@ -37,9 +41,9 @@ def tile_attention_pa_kernel(tc, x, w_q, w_k, out):
 
     with ExitStack() as ctx:
         consts = ctx.enter_context(tc.tile_pool(name="consts", bufs=1))
-        raw_pool = ctx.enter_context(tc.tile_pool(name="raw", bufs=HALVES * (1 + 2 * HEADS)))
+        raw_pool = ctx.enter_context(tc.tile_pool(name="raw", bufs=RAW_BUFS))
         stage = ctx.enter_context(tc.tile_pool(name="stage", bufs=6))
-        w_pool = ctx.enter_context(tc.tile_pool(name="w", bufs=3))
+        w_pool = ctx.enter_context(tc.tile_pool(name="w", bufs=4))
         qk_pool = ctx.enter_context(tc.tile_pool(name="qk", bufs=2))
         out_pool = ctx.enter_context(tc.tile_pool(name="outs", bufs=3))
         turn_psum = ctx.enter_context(tc.psum_pool(name="turn", bufs=4))
@@ -48,8 +52,7 @@ def tile_attention_pa_kernel(tc, x, w_q, w_k, out):
 
         ident = consts.tile([P, P], F32)
         make_identity(nc, ident[:])
-        x_codes = consts.tile([P, PASSES, TOKENS], U32, align_bytes=64)
-        x_scales = consts.tile([P, PASSES, TOKENS], U8, align_bytes=64)
+        x_pack = consts.tile([P, PASSES, X_ROW], U32, align_bytes=64)
 
         zeros = consts.tile([P, HEAD], BF16)
         nc.vector.memset(zeros[:], 0.0)
@@ -59,39 +62,13 @@ def tile_attention_pa_kernel(tc, x, w_q, w_k, out):
                 spare = acc_psum.tile([P, HEAD], F32, name="acc")
                 nc.tensor.matmul(spare[:], zeros[:, :P], zeros[:], start=True, stop=True)
 
-        def load(rows):
-            raw = raw_pool.tile([P, SLOTS, MODEL], BF16)
-            nc.sync.dma_start(out=raw[:], in_=rows)
+        def load(rows, pieces=1):
+            raw = raw_pool.tile([P, SLOTS, MODEL], BF16, align_bytes=64, name="raw")
+            width = MODEL // pieces
+            for c in range(pieces):
+                cols = slice(c * width, (c + 1) * width)
+                nc.sync.dma_start(out=raw[:, :, cols], in_=rows[:, :, cols])
             return raw
-
-        def transpose_and_quantise(raw, codes, scales):
-            for g in range(PASSES):
-                turned = turn_psum.tile([P, SLOTS, WORD_PLANES, P], F32)
-                for s in range(SLOTS):
-                    words = raw[:, s, :].bitcast(F32)
-                    for u in range(WORD_PLANES):
-                        first = (WORD_PLANES * g + u) * P
-                        nc.tensor.transpose(turned[:, s, u, :], words[:, first : first + P], ident[:])
-                grouped = stage.tile([P, UNIT * PACK], BF16, align_bytes=64)
-                nc.scalar.copy(
-                    out=grouped[:].bitcast(F32).rearrange("p (s r u) -> p s r u", s=SLOTS, u=WORD_PLANES),
-                    in_=turned[:].rearrange("p s u r -> p s r u"),
-                )
-                nc.vector.quantize_mx(out=codes[:, g, :].bitcast(FP8X4), scales=scales[:, g, :], in_=grouped[:])
-
-        def project(acc, lhs, lhs_cols, rhs, rhs_cols):
-            lhs_codes, lhs_scales = lhs
-            rhs_codes, rhs_scales = rhs
-            for g in range(PASSES):
-                nc.tensor.matmul_mx(
-                    out=acc,
-                    lhsT=lhs_codes[:, g, lhs_cols].bitcast(FP8X4),
-                    lhsT_scale=lhs_scales[:, g, lhs_cols],
-                    rhs=rhs_codes[:, g, rhs_cols].bitcast(FP8X4),
-                    rhs_scale=rhs_scales[:, g, rhs_cols],
-                    start=(g == 0),
-                    stop=(g == PASSES - 1),
-                )
 
         def slot_cols(t):
             return slice(t * P, (t + 1) * P)
@@ -99,27 +76,70 @@ def tile_attention_pa_kernel(tc, x, w_q, w_k, out):
         def unit_cols(half):
             return slice(half * UNIT, (half + 1) * UNIT)
 
-        x_mx = (x_codes, x_scales)
+        def views(tile, width):
+            return (lambda g: tile[:, g, :width], lambda g: tile[:, g, width:].bitcast(U8))
 
-        def project_q(w_mx, q_grouped, half):
-            for token_half in range(HALVES):
-                acc = acc_psum.tile([P, SLOTS, UNIT], F32, name="acc")
+        def columns(mx, cols):
+            codes, scales = mx
+            return (lambda g: codes(g)[:, cols], lambda g: scales(g)[:, cols])
+
+        def transpose_and_quantise(raw, mx, vector_copies=()):
+            codes, scales = mx
+
+            def quantise(g, grouped):
+                nc.vector.quantize_mx(out=codes(g).bitcast(FP8X4), scales=scales(g), in_=grouped[:])
+
+            waiting_tile = None
+            for g in range(PASSES):
+                turned = turn_psum.tile([P, SLOTS, WORD_PLANES, P], F32, name="turned")
                 for s in range(SLOTS):
-                    project(acc[:, s, :], w_mx, slot_cols(s), x_mx, unit_cols(token_half))
-                nc.vector.tensor_copy(
-                    out=q_grouped[:, unit_cols(token_half), SLOTS * half : SLOTS * (half + 1)],
-                    in_=acc[:].rearrange("p s n -> p n s"),
+                    words = raw[:, s, :].bitcast(F32)
+                    for u in range(WORD_PLANES):
+                        first = (WORD_PLANES * g + u) * P
+                        nc.tensor.transpose(turned[:, s, u, :], words[:, first : first + P], ident[:])
+                grouped = stage.tile([P, UNIT * PACK], BF16, align_bytes=64, name="grouped")
+                (nc.vector.tensor_copy if g in vector_copies else nc.scalar.copy)(
+                    out=grouped[:].bitcast(F32).rearrange("p (s r u) -> p s r u", s=SLOTS, u=WORD_PLANES),
+                    in_=turned[:].rearrange("p s u r -> p s r u"),
+                )
+                if waiting_tile is not None:
+                    quantise(g - 1, waiting_tile)
+                waiting_tile = grouped
+            quantise(PASSES - 1, waiting_tile)
+
+        def project(acc, lhs, rhs):
+            lhs_codes, lhs_scales = lhs
+            rhs_codes, rhs_scales = rhs
+            for g in range(PASSES):
+                nc.tensor.matmul_mx(
+                    out=acc,
+                    lhsT=lhs_codes(g).bitcast(FP8X4),
+                    lhsT_scale=lhs_scales(g),
+                    rhs=rhs_codes(g).bitcast(FP8X4),
+                    rhs_scale=rhs_scales(g),
+                    start=(g == 0),
+                    stop=(g == PASSES - 1),
                 )
 
-        def project_k(w_mx, k_grouped):
-            for pair in range(PACK // SLOTS):
-                acc = acc_psum.tile([P, SLOTS, UNIT], F32, name="acc")
-                for s in range(SLOTS):
-                    project(acc[:, s, :], x_mx, slot_cols(SLOTS * pair + s), w_mx, unit_cols(0))
-                nc.vector.tensor_copy(
-                    out=k_grouped[:, :, SLOTS * pair : SLOTS * (pair + 1)],
-                    in_=acc[:].rearrange("p s m -> p m s"),
-                )
+        x_mx = views(x_pack, TOKENS)
+
+        def project_q_half(w_mx, q_grouped, half, token_half):
+            acc = acc_psum.tile([P, SLOTS, UNIT], F32, name="acc")
+            for s in range(SLOTS):
+                project(acc[:, s, :], columns(w_mx, slot_cols(s)), columns(x_mx, unit_cols(token_half)))
+            (nc.scalar.copy if token_half in S_COPY_Q else nc.vector.tensor_copy)(
+                out=q_grouped[:, unit_cols(token_half), SLOTS * half : SLOTS * (half + 1)],
+                in_=acc[:].rearrange("p s n -> p n s"),
+            )
+
+        def project_k_pair(w_mx, k_grouped, pair):
+            acc = acc_psum.tile([P, SLOTS, UNIT], F32, name="acc")
+            for s in range(SLOTS):
+                project(acc[:, s, :], columns(x_mx, slot_cols(SLOTS * pair + s)), w_mx)
+            (nc.scalar.copy if pair in S_COPY_K else nc.vector.tensor_copy)(
+                out=k_grouped[:, :, SLOTS * pair : SLOTS * (pair + 1)],
+                in_=acc[:].rearrange("p s m -> p m s"),
+            )
 
         def quantise_grouped(grouped, width):
             codes = qk_pool.tile([P, width], U32, align_bytes=64, name="codes%d" % width)
@@ -129,10 +149,10 @@ def tile_attention_pa_kernel(tc, x, w_q, w_k, out):
             )
             return codes, scales
 
-        def logits(q_mx, k_mx, h, half):
+        def logits(q_mx, k_mx, h, half, copies=(nc.scalar.copy, nc.scalar.copy)):
             q_codes, q_scales = q_mx
             k_codes, k_scales = k_mx
-            result = out_pool.tile([P, PACK, UNIT], F32)
+            result = out_pool.tile([P, PACK, UNIT], F32, name="result")
             for pair in range(PACK // SLOTS):
                 acc = acc_psum.tile([P, SLOTS, UNIT], F32, name="acc")
                 for s in range(SLOTS):
@@ -146,50 +166,93 @@ def tile_attention_pa_kernel(tc, x, w_q, w_k, out):
                         start=True,
                         stop=True,
                     )
-                nc.scalar.copy(out=result[:, SLOTS * pair : SLOTS * (pair + 1), :], in_=acc[:])
+                copies[pair](out=result[:, SLOTS * pair : SLOTS * (pair + 1), :], in_=acc[:])
             nc.sync.dma_start(out=out_rows[h][:, :, unit_cols(half)], in_=result[:])
 
-        x_raw = [load(x_units[half]) for half in range(HALVES)]
-        units = []
+        def finish(w_mx, q_mx, h, half, waiting):
+            q_codes, q_scales = q_mx
+            parts = []
+            for part in range(SLOTS):
+                acc = acc_psum.tile([P, PACK, P], F32, name="acc")
+                for t in range(PACK):
+                    project(acc[:, t, :], columns(x_mx, slot_cols(t)), columns(w_mx, slot_cols(part)))
+                grouped = qk_pool.tile([P, P, PACK], BF16, align_bytes=64, name="part_grouped")
+                nc.vector.tensor_copy(out=grouped[:], in_=acc[:].rearrange("p t m -> p m t"))
+                parts.append(quantise_grouped(grouped, P))
+            both = (nc.scalar.copy, nc.vector.tensor_copy)
+            logits(*waiting, copies=both)
+            for part, (k_codes, k_scales) in enumerate(parts):
+                acc = acc_psum.tile([P, PACK, P], F32, name="acc")
+                for t in range(PACK):
+                    nc.tensor.matmul_mx(
+                        out=acc[:, t, :],
+                        lhsT=q_codes[:, slot_cols(t)].bitcast(FP8X4),
+                        lhsT_scale=q_scales[:, slot_cols(t)],
+                        rhs=k_codes[:].bitcast(FP8X4),
+                        rhs_scale=k_scales[:],
+                        start=True,
+                        stop=True,
+                    )
+                result = out_pool.tile([P, PACK, P], F32, name="part_result")
+                both[part](out=result[:], in_=acc[:])
+                first = half * UNIT + part * P
+                nc.sync.dma_start(out=out_rows[h][:, :, first : first + P], in_=result[:])
+
+        order = []
         for h in range(HEADS):
-            for half in range(HALVES):
-                units.append((True, h, half, load(q_units[h, half])))
-            for half in range(HALVES):
-                units.append((False, h, half, load(k_units[h, half])))
+            order += [(True, h, 0), (True, h, 1), (False, h, 0), (False, h, 1)]
+        raws = {}
 
-        def prepare(unit):
-            w_codes = w_pool.tile([P, PASSES, UNIT], U32, align_bytes=64)
-            w_scales = w_pool.tile([P, PASSES, UNIT], U8, align_bytes=64)
-            transpose_and_quantise(unit[3], w_codes, w_scales)
-            return w_codes, w_scales
+        def load_unit(i, pieces=1):
+            is_q, h, half = order[i]
+            raws[i] = load((q_units if is_q else k_units)[h, half], pieces)
 
-        keep_warm(WARM_START)
-        for half in range(HALVES):
-            transpose_and_quantise(x_raw[half], x_codes[:, :, unit_cols(half)], x_scales[:, :, unit_cols(half)])
-            keep_warm(WARM_UNIT)
+        def prepare(i, vector_copies=()):
+            tile = w_pool.tile([P, PASSES, UNIT + UNIT // 4], U32, align_bytes=64, name="w_pack")
+            mx = views(tile, UNIT)
+            transpose_and_quantise(raws[i], mx, vector_copies)
+            return mx
 
-        ready = prepare(units[0])
-        keep_warm(WARM_UNIT)
+        x_raw = [load(x_units[0], 4)]
+        load_unit(0, 2)
+        x_raw.append(load(x_units[1], 2))
+        for i in range(1, len(order)):
+            load_unit(i)
+        keep_warm(WARM[0])
+        transpose_and_quantise(x_raw[0], columns(x_mx, unit_cols(0)), SHARE)
+        keep_warm(WARM[1])
+        w_mx = prepare(0, SHARE)
+        transpose_and_quantise(x_raw[1], columns(x_mx, unit_cols(1)), SHARE)
+        q_grouped = qk_pool.tile([P, TOKENS, PACK], BF16, align_bytes=64, name="q_grouped")
+        project_q_half(w_mx, q_grouped, 0, 0)
+        ready = w_mx
         waiting = None
-        q_grouped = None
         q_mx = None
-        for i, (is_q, h, half, raw) in enumerate(units):
+        for i, (is_q, h, half) in enumerate(order):
             w_mx = ready
-            if i + 1 < len(units):
-                ready = prepare(units[i + 1])
+            if i == 0:
+                project_q_half(w_mx, q_grouped, 0, 1)
+                ready = prepare(1, SHARE)
+                continue
+            if i + 1 < len(order):
+                ready = prepare(i + 1)
             if is_q:
                 if half == 0:
-                    q_grouped = qk_pool.tile([P, TOKENS, PACK], BF16, align_bytes=64)
-                project_q(w_mx, q_grouped, half)
+                    q_grouped = qk_pool.tile([P, TOKENS, PACK], BF16, align_bytes=64, name="q_grouped")
+                for token_half in range(HALVES):
+                    project_q_half(w_mx, q_grouped, half, token_half)
                 if half == HALVES - 1:
                     q_mx = quantise_grouped(q_grouped, TOKENS)
+            elif i == len(order) - 1:
+                finish(w_mx, q_mx, h, half, waiting)
+                break
             else:
-                k_grouped = qk_pool.tile([P, UNIT, PACK], BF16, align_bytes=64)
-                project_k(w_mx, k_grouped)
+                k_grouped = qk_pool.tile([P, UNIT, PACK], BF16, align_bytes=64, name="k_grouped")
+                for pair in range(PACK // SLOTS):
+                    project_k_pair(w_mx, k_grouped, pair)
                 k_mx = quantise_grouped(k_grouped, UNIT)
             if waiting is not None:
                 logits(*waiting)
                 waiting = None
             if not is_q:
                 waiting = (q_mx, k_mx, h, half)
-        logits(*waiting)

@@ -25,7 +25,7 @@ RAW_BUFS = 18
 SHARE = (1,)
 S_COPY_K = ()
 S_COPY_Q = ()
-WARM = (6, 0)
+WARM = (6, 1)
 WORD_PLANES = 2
 
 FLOPS = 2 * 2 * TOKENS * MODEL * HEADS * HEAD + 2 * HEADS * TOKENS * HEAD * TOKENS
@@ -83,7 +83,7 @@ def tile_attention_pa_kernel(tc, x, w_q, w_k, out):
             codes, scales = mx
             return (lambda g: codes(g)[:, cols], lambda g: scales(g)[:, cols])
 
-        def transpose_and_quantise(raw, mx, vector_copies=()):
+        def transpose_and_quantise(raw, mx, vector_copies=(), warm=0):
             codes, scales = mx
 
             def quantise(g, grouped):
@@ -97,6 +97,8 @@ def tile_attention_pa_kernel(tc, x, w_q, w_k, out):
                     for u in range(WORD_PLANES):
                         first = (WORD_PLANES * g + u) * P
                         nc.tensor.transpose(turned[:, s, u, :], words[:, first : first + P], ident[:])
+                if g % 2 == 1:
+                    keep_warm(warm)
                 grouped = stage.tile([P, UNIT * PACK], BF16, align_bytes=64, name="grouped")
                 (nc.vector.tensor_copy if g in vector_copies else nc.scalar.copy)(
                     out=grouped[:].bitcast(F32).rearrange("p (s r u) -> p s r u", s=SLOTS, u=WORD_PLANES),
@@ -207,10 +209,10 @@ def tile_attention_pa_kernel(tc, x, w_q, w_k, out):
             is_q, h, half = order[i]
             raws[i] = load((q_units if is_q else k_units)[h, half], pieces)
 
-        def prepare(i, vector_copies=()):
+        def prepare(i, vector_copies=(), warm=0):
             tile = w_pool.tile([P, PASSES, UNIT + UNIT // 4], U32, align_bytes=64, name="w_pack")
             mx = views(tile, UNIT)
-            transpose_and_quantise(raws[i], mx, vector_copies)
+            transpose_and_quantise(raws[i], mx, vector_copies, warm)
             return mx
 
         x_raw = [load(x_units[0], 4)]
@@ -219,10 +221,9 @@ def tile_attention_pa_kernel(tc, x, w_q, w_k, out):
         for i in range(1, len(order)):
             load_unit(i)
         keep_warm(WARM[0])
-        transpose_and_quantise(x_raw[0], columns(x_mx, unit_cols(0)), SHARE)
-        keep_warm(WARM[1])
-        w_mx = prepare(0, SHARE)
-        transpose_and_quantise(x_raw[1], columns(x_mx, unit_cols(1)), SHARE)
+        transpose_and_quantise(x_raw[0], columns(x_mx, unit_cols(0)), SHARE, WARM[1])
+        w_mx = prepare(0, SHARE, WARM[1])
+        transpose_and_quantise(x_raw[1], columns(x_mx, unit_cols(1)), SHARE, WARM[1])
         q_grouped = qk_pool.tile([P, TOKENS, PACK], BF16, align_bytes=64, name="q_grouped")
         project_q_half(w_mx, q_grouped, 0, 0)
         ready = w_mx
@@ -231,8 +232,8 @@ def tile_attention_pa_kernel(tc, x, w_q, w_k, out):
         for i, (is_q, h, half) in enumerate(order):
             w_mx = ready
             if i == 0:
-                project_q_half(w_mx, q_grouped, 0, 1)
                 ready = prepare(1, SHARE)
+                project_q_half(w_mx, q_grouped, 0, 1)
                 continue
             if i + 1 < len(order):
                 ready = prepare(i + 1)

@@ -23,7 +23,8 @@ X_ROW = TOKENS + TOKENS // 4
 HALVES = HEAD // UNIT
 RAW_BUFS = 18
 SHARE = (1,)
-S_COPY_K = ()
+PAUSES = (2,)
+S_COPY_K = (1,)
 S_COPY_Q = ()
 WARM = (6, 1)
 WORD_PLANES = 2
@@ -83,7 +84,7 @@ def tile_attention_pa_kernel(tc, x, w_q, w_k, out):
             codes, scales = mx
             return (lambda g: codes(g)[:, cols], lambda g: scales(g)[:, cols])
 
-        def transpose_and_quantise(raw, mx, vector_copies=(), warm=0):
+        def transpose_and_quantise(raw, mx, vector_copies=(), warm=0, pauses=(), between=None):
             codes, scales = mx
 
             def quantise(g, grouped):
@@ -91,6 +92,8 @@ def tile_attention_pa_kernel(tc, x, w_q, w_k, out):
 
             waiting_tile = None
             for g in range(PASSES):
+                if g in pauses:
+                    between()
                 turned = turn_psum.tile([P, SLOTS, WORD_PLANES, P], F32, name="turned")
                 for s in range(SLOTS):
                     words = raw[:, s, :].bitcast(F32)
@@ -209,10 +212,10 @@ def tile_attention_pa_kernel(tc, x, w_q, w_k, out):
             is_q, h, half = order[i]
             raws[i] = load((q_units if is_q else k_units)[h, half], pieces)
 
-        def prepare(i, vector_copies=(), warm=0):
+        def prepare(i, vector_copies=(), warm=0, pauses=(), between=None):
             tile = w_pool.tile([P, PASSES, UNIT + UNIT // 4], U32, align_bytes=64, name="w_pack")
             mx = views(tile, UNIT)
-            transpose_and_quantise(raws[i], mx, vector_copies, warm)
+            transpose_and_quantise(raws[i], mx, vector_copies, warm, pauses, between)
             return mx
 
         x_raw = [load(x_units[0], 4)]
@@ -235,22 +238,21 @@ def tile_attention_pa_kernel(tc, x, w_q, w_k, out):
                 ready = prepare(1, SHARE)
                 project_q_half(w_mx, q_grouped, 0, 1)
                 continue
-            if i + 1 < len(order):
-                ready = prepare(i + 1)
+            if i == len(order) - 1:
+                finish(w_mx, q_mx, h, half, waiting)
+                break
             if is_q:
                 if half == 0:
                     q_grouped = qk_pool.tile([P, TOKENS, PACK], BF16, align_bytes=64, name="q_grouped")
-                for token_half in range(HALVES):
-                    project_q_half(w_mx, q_grouped, half, token_half)
-                if half == HALVES - 1:
-                    q_mx = quantise_grouped(q_grouped, TOKENS)
-            elif i == len(order) - 1:
-                finish(w_mx, q_mx, h, half, waiting)
-                break
+                step = lambda part: project_q_half(w_mx, q_grouped, half, part)
             else:
                 k_grouped = qk_pool.tile([P, UNIT, PACK], BF16, align_bytes=64, name="k_grouped")
-                for pair in range(PACK // SLOTS):
-                    project_k_pair(w_mx, k_grouped, pair)
+                step = lambda part: project_k_pair(w_mx, k_grouped, part)
+            ready = prepare(i + 1, pauses=PAUSES, between=lambda: step(0))
+            step(1)
+            if is_q and half == HALVES - 1:
+                q_mx = quantise_grouped(q_grouped, TOKENS)
+            if not is_q:
                 k_mx = quantise_grouped(k_grouped, UNIT)
             if waiting is not None:
                 logits(*waiting)

from contextlib import ExitStack

import concourse.mybir as mybir
from concourse.masks import make_identity

BF16 = mybir.dt.bfloat16
F32 = mybir.dt.float32
U32 = mybir.dt.uint32
U8 = mybir.dt.uint8
FP8X4 = mybir.dt.float8_e4m3fn_x4

P = 128
PACK = 4
K_PASS = P * PACK
TOKENS = 512
MODEL = 2048
HEADS = 4
HEAD = 512
PASSES = MODEL // K_PASS
SLOTS = 2
UNIT = SLOTS * P
X_ROW = TOKENS + TOKENS // 4
HALVES = HEAD // UNIT
RAW_BUFS = 18
SHARE = (1,)
PAUSES = (2,)
S_COPY_K = (1,)
S_COPY_Q = ()
WARM = (6, 1)
WORD_PLANES = 2

FLOPS = 2 * 2 * TOKENS * MODEL * HEADS * HEAD + 2 * HEADS * TOKENS * HEAD * TOKENS


def tile_attention_pa_kernel(tc, x, w_q, w_k, out):
    nc = tc.nc

    x_units = x[0].rearrange("(p half s) e -> half p s e", half=HALVES, s=SLOTS)
    q_units = w_q.rearrange("(h p half s) e -> h half p s e", h=HEADS, half=HALVES, s=SLOTS)
    k_units = w_k.rearrange("(h half s p) e -> h half p s e", h=HEADS, half=HALVES, s=SLOTS)
    out_rows = out[0].rearrange("h (c t) m -> h c t m", t=PACK)

    with ExitStack() as ctx:
        consts = ctx.enter_context(tc.tile_pool(name="consts", bufs=1))
        raw_pool = ctx.enter_context(tc.tile_pool(name="raw", bufs=RAW_BUFS))
        stage = ctx.enter_context(tc.tile_pool(name="stage", bufs=6))
        w_pool = ctx.enter_context(tc.tile_pool(name="w", bufs=4))
        qk_pool = ctx.enter_context(tc.tile_pool(name="qk", bufs=2))
        out_pool = ctx.enter_context(tc.tile_pool(name="outs", bufs=3))
        turn_psum = ctx.enter_context(tc.psum_pool(name="turn", bufs=4))
        acc_psum = ctx.enter_context(tc.psum_pool(name="acc", bufs=4))
        ctx.enter_context(tc.manual_schedule())

        ident = consts.tile([P, P], F32)
        make_identity(nc, ident[:])
        x_pack = consts.tile([P, PASSES, X_ROW], U32, align_bytes=64)

        zeros = consts.tile([P, HEAD], BF16)
        nc.vector.memset(zeros[:], 0.0)

        def keep_warm(count):
            for c in range(count):
                spare = acc_psum.tile([P, HEAD], F32, name="acc")
                nc.tensor.matmul(spare[:], zeros[:, :P], zeros[:], start=True, stop=True)

        def load(rows, pieces=1):
            raw = raw_pool.tile([P, SLOTS, MODEL], BF16, align_bytes=64, name="raw")
            width = MODEL // pieces
            for c in range(pieces):
                cols = slice(c * width, (c + 1) * width)
                nc.sync.dma_start(out=raw[:, :, cols], in_=rows[:, :, cols])
            return raw

        def slot_cols(t):
            return slice(t * P, (t + 1) * P)

        def unit_cols(half):
            return slice(half * UNIT, (half + 1) * UNIT)

        def views(tile, width):
            return (lambda g: tile[:, g, :width], lambda g: tile[:, g, width:].bitcast(U8))

        def columns(mx, cols):
            codes, scales = mx
            return (lambda g: codes(g)[:, cols], lambda g: scales(g)[:, cols])

        def transpose_and_quantise(raw, mx, vector_copies=(), warm=0, pauses=(), between=None):
            codes, scales = mx

            def quantise(g, grouped):
                nc.vector.quantize_mx(out=codes(g).bitcast(FP8X4), scales=scales(g), in_=grouped[:])

            waiting_tile = None
            for g in range(PASSES):
                if g in pauses:
                    between()
                turned = turn_psum.tile([P, SLOTS, WORD_PLANES, P], F32, name="turned")
                for s in range(SLOTS):
                    words = raw[:, s, :].bitcast(F32)
                    for u in range(WORD_PLANES):
                        first = (WORD_PLANES * g + u) * P
                        nc.tensor.transpose(turned[:, s, u, :], words[:, first : first + P], ident[:])
                if g % 2 == 1:
                    keep_warm(warm)
                grouped = stage.tile([P, UNIT * PACK], BF16, align_bytes=64, name="grouped")
                (nc.vector.tensor_copy if g in vector_copies else nc.scalar.copy)(
                    out=grouped[:].bitcast(F32).rearrange("p (s r u) -> p s r u", s=SLOTS, u=WORD_PLANES),
                    in_=turned[:].rearrange("p s u r -> p s r u"),
                )
                if waiting_tile is not None:
                    quantise(g - 1, waiting_tile)
                waiting_tile = grouped
            quantise(PASSES - 1, waiting_tile)

        def project(acc, lhs, rhs):
            lhs_codes, lhs_scales = lhs
            rhs_codes, rhs_scales = rhs
            for g in range(PASSES):
                nc.tensor.matmul_mx(
                    out=acc,
                    lhsT=lhs_codes(g).bitcast(FP8X4),
                    lhsT_scale=lhs_scales(g),
                    rhs=rhs_codes(g).bitcast(FP8X4),
                    rhs_scale=rhs_scales(g),
                    start=(g == 0),
                    stop=(g == PASSES - 1),
                )

        x_mx = views(x_pack, TOKENS)

        def project_q_half(w_mx, q_grouped, half, token_half):
            acc = acc_psum.tile([P, SLOTS, UNIT], F32, name="acc")
            for s in range(SLOTS):
                project(acc[:, s, :], columns(w_mx, slot_cols(s)), columns(x_mx, unit_cols(token_half)))
            (nc.scalar.copy if token_half in S_COPY_Q else nc.vector.tensor_copy)(
                out=q_grouped[:, unit_cols(token_half), SLOTS * half : SLOTS * (half + 1)],
                in_=acc[:].rearrange("p s n -> p n s"),
            )

        def project_k_pair(w_mx, k_grouped, pair):
            acc = acc_psum.tile([P, SLOTS, UNIT], F32, name="acc")
            for s in range(SLOTS):
                project(acc[:, s, :], columns(x_mx, slot_cols(SLOTS * pair + s)), w_mx)
            (nc.scalar.copy if pair in S_COPY_K else nc.vector.tensor_copy)(
                out=k_grouped[:, :, SLOTS * pair : SLOTS * (pair + 1)],
                in_=acc[:].rearrange("p s m -> p m s"),
            )

        def quantise_grouped(grouped, width):
            codes = qk_pool.tile([P, width], U32, align_bytes=64, name="codes%d" % width)
            scales = qk_pool.tile([P, width], U8, align_bytes=64, name="scales%d" % width)
            nc.vector.quantize_mx(
                out=codes[:].bitcast(FP8X4), scales=scales[:], in_=grouped[:].rearrange("p n t -> p (n t)")
            )
            return codes, scales

        def logits(q_mx, k_mx, h, half, copies=(nc.scalar.copy, nc.scalar.copy)):
            q_codes, q_scales = q_mx
            k_codes, k_scales = k_mx
            result = out_pool.tile([P, PACK, UNIT], F32, name="result")
            for pair in range(PACK // SLOTS):
                acc = acc_psum.tile([P, SLOTS, UNIT], F32, name="acc")
                for s in range(SLOTS):
                    cols = slot_cols(SLOTS * pair + s)
                    nc.tensor.matmul_mx(
                        out=acc[:, s, :],
                        lhsT=q_codes[:, cols].bitcast(FP8X4),
                        lhsT_scale=q_scales[:, cols],
                        rhs=k_codes[:].bitcast(FP8X4),
                        rhs_scale=k_scales[:],
                        start=True,
                        stop=True,
                    )
                copies[pair](out=result[:, SLOTS * pair : SLOTS * (pair + 1), :], in_=acc[:])
            nc.sync.dma_start(out=out_rows[h][:, :, unit_cols(half)], in_=result[:])

        def finish(w_mx, q_mx, h, half, waiting):
            q_codes, q_scales = q_mx
            parts = []
            for part in range(SLOTS):
                acc = acc_psum.tile([P, PACK, P], F32, name="acc")
                for t in range(PACK):
                    project(acc[:, t, :], columns(x_mx, slot_cols(t)), columns(w_mx, slot_cols(part)))
                grouped = qk_pool.tile([P, P, PACK], BF16, align_bytes=64, name="part_grouped")
                nc.vector.tensor_copy(out=grouped[:], in_=acc[:].rearrange("p t m -> p m t"))
                parts.append(quantise_grouped(grouped, P))
            both = (nc.scalar.copy, nc.vector.tensor_copy)
            logits(*waiting, copies=both)
            for part, (k_codes, k_scales) in enumerate(parts):
                acc = acc_psum.tile([P, PACK, P], F32, name="acc")
                for t in range(PACK):
                    nc.tensor.matmul_mx(
                        out=acc[:, t, :],
                        lhsT=q_codes[:, slot_cols(t)].bitcast(FP8X4),
                        lhsT_scale=q_scales[:, slot_cols(t)],
                        rhs=k_codes[:].bitcast(FP8X4),
                        rhs_scale=k_scales[:],
                        start=True,
                        stop=True,
                    )
                result = out_pool.tile([P, PACK, P], F32, name="part_result")
                both[part](out=result[:], in_=acc[:])
                first = half * UNIT + part * P
                nc.sync.dma_start(out=out_rows[h][:, :, first : first + P], in_=result[:])

        order = []
        for h in range(HEADS):
            order += [(True, h, 0), (True, h, 1), (False, h, 0), (False, h, 1)]
        raws = {}

        def load_unit(i, pieces=1):
            is_q, h, half = order[i]
            raws[i] = load((q_units if is_q else k_units)[h, half], pieces)

        def prepare(i, vector_copies=(), warm=0, pauses=(), between=None):
            tile = w_pool.tile([P, PASSES, UNIT + UNIT // 4], U32, align_bytes=64, name="w_pack")
            mx = views(tile, UNIT)
            transpose_and_quantise(raws[i], mx, vector_copies, warm, pauses, between)
            return mx

        x_raw = [load(x_units[0], 4)]
        load_unit(0, 2)
        x_raw.append(load(x_units[1], 2))
        for i in range(1, len(order)):
            load_unit(i)
        keep_warm(WARM[0])
        transpose_and_quantise(x_raw[0], columns(x_mx, unit_cols(0)), SHARE, WARM[1])
        w_mx = prepare(0, SHARE, WARM[1])
        transpose_and_quantise(x_raw[1], columns(x_mx, unit_cols(1)), SHARE, WARM[1])
        q_grouped = qk_pool.tile([P, TOKENS, PACK], BF16, align_bytes=64, name="q_grouped")
        project_q_half(w_mx, q_grouped, 0, 0)
        ready = w_mx
        waiting = None
        q_mx = None
        for i, (is_q, h, half) in enumerate(order):
            w_mx = ready
            if i == 0:
                ready = prepare(1, SHARE)
                project_q_half(w_mx, q_grouped, 0, 1)
                continue
            if i == len(order) - 1:
                finish(w_mx, q_mx, h, half, waiting)
                break
            if is_q:
                if half == 0:
                    q_grouped = qk_pool.tile([P, TOKENS, PACK], BF16, align_bytes=64, name="q_grouped")
                step = lambda part: project_q_half(w_mx, q_grouped, half, part)
            else:
                k_grouped = qk_pool.tile([P, UNIT, PACK], BF16, align_bytes=64, name="k_grouped")
                step = lambda part: project_k_pair(w_mx, k_grouped, part)
            ready = prepare(i + 1, pauses=PAUSES, between=lambda: step(0))
            step(1)
            if is_q and half == HALVES - 1:
                q_mx = quantise_grouped(q_grouped, TOKENS)
            if not is_q:
                k_mx = quantise_grouped(k_grouped, UNIT)
            if waiting is not None:
                logits(*waiting)
                waiting = None
            if not is_q:
                waiting = (q_mx, k_mx, h, half)
